import numpy as np
import ml_dtypes


def mxq(x, axis, fmt="e4m3"):
    dtype, down = {"e4m3": (ml_dtypes.float8_e4m3fn, 7), "e5m2": (ml_dtypes.float8_e5m2, 14)}[fmt]
    v = np.moveaxis(np.asarray(x, np.float32).astype(ml_dtypes.bfloat16).astype(np.float64), axis, -1)
    blocks = v.reshape(v.shape[:-1] + (-1, 32))
    amax = np.abs(blocks).max(-1, keepdims=True)
    byte = np.maximum(np.where(amax > 0, np.frexp(amax)[1] - 1 + 127, 0) - down, 1)
    scale = np.exp2(byte - 127.0)
    codes = (blocks / scale).astype(np.float32).astype(dtype).astype(np.float64)
    return np.moveaxis((codes * scale).reshape(v.shape), -1, axis)


WIDE = False


def mx_kscale(k):
    if not WIDE:
        return np.ones(k)
    levels = np.array([20, -20, 10, -10, 0])
    a = np.random.permutation(np.resize(levels, k // 512 * 4)).reshape(k // 512, 4)
    idx = np.arange(k)
    return np.exp2(a[idx // 512, idx % 128 // 32])


BF16 = ml_dtypes.bfloat16


def bf(x):
    return np.asarray(x, np.float32).astype(BF16)


def f64(x):
    return np.asarray(x).astype(np.float64)


B, L, S, D, DA, H, MLP = 2, 3, 256, 1024, 1024, 16, 4096
T = B * S
EPS = 1e-5


def layer_norm(u, g, b):
    mu = u.mean(-1, keepdims=True)
    var = ((u - mu) ** 2).mean(-1, keepdims=True)
    return (u - mu) / np.sqrt(var + EPS) * g + b


def setup_inputs():
    s = np.asarray(mx_kscale(T)).reshape(B, S, 1)
    r = np.random.standard_normal
    h0 = bf(r((B, S, DA)) * 2.0)
    x = bf(r((B, S, D)))
    w = bf(r((DA, D)) * 0.5 / np.sqrt(DA))
    b = bf(r(D) * 0.2)
    ng = bf(1.0 + 0.1 * r(D))
    nb = bf(r(D) * 0.1)
    g = bf(r((B, S, D)) * np.exp2(np.random.randint(-12, 1, (B, S, 1))) / s)
    o = f64(h0) @ f64(w) + f64(b)
    mu = o.mean(-1, keepdims=True)
    var = ((o - mu) ** 2).mean(-1, keepdims=True)
    rstd = 1.0 / np.sqrt(var + EPS)
    return {"h_attn": bf(f64(h0) * s), "x": x, "attn_out_W": w, "attn_out_b": b,
            "attn_norm_g": ng, "attn_norm_b": nb,
            "o": np.asarray(o, np.float32), "mu": np.asarray(mu, np.float32),
            "rstd": np.asarray(rstd, np.float32), "grad_out": g}


def reference(h_attn, x, attn_out_W, attn_out_b, attn_norm_g, attn_norm_b, o, mu, rstd, grad_out):
    rs = f64(rstd)
    xhat = (f64(o) - f64(mu)) * rs
    gy = f64(grad_out) * f64(attn_norm_g)
    m1 = gy.mean(-1, keepdims=True)
    m2 = (gy * xhat).mean(-1, keepdims=True)
    do = rs * (gy - m1 - xhat * m2)
    h2 = f64(h_attn).reshape(T, DA)
    do2 = do.reshape(T, D)
    return mxq(h2, 0, "e4m3").T @ mxq(do2, 0, "e5m2")

@@ -1,0 +1,270 @@
+import concourse.mybir as mybir
+
+F32 = mybir.dt.float32
+BF16 = mybir.dt.bfloat16
+U32 = mybir.dt.uint32
+U8 = mybir.dt.uint8
+E4M3_X4 = mybir.dt.float8_e4m3fn_x4
+E5M2_X4 = mybir.dt.float8_e5m2_x4
+ALU = mybir.AluOpType
+ACT = mybir.ActivationFunctionType
+
+P = 128
+PACK = 4
+TOKENS = P * PACK
+DA = 1024
+D = 1024
+M_TILE = 128
+N_TILE = 512
+M_TILES = DA // M_TILE
+N_TILES = D // N_TILE
+
+FLOPS = 2 * TOKENS * DA * D
+BYTES = 2 * TOKENS * DA + 2 * TOKENS * D + 4 * TOKENS * D + 2 * D + 8 * TOKENS + 4 * DA * D
+
+
+def tile_dcadecoderblock_pb_v_kernel(
+    tc, h_attn, x, attn_out_W, attn_out_b, attn_norm_g, attn_norm_b, o, mu, rstd, grad_out, out
+):
+    nc = tc.nc
+
+    h_rows = h_attn.flatten_outer_dims().rearrange("(p j) c -> p j c", j=PACK)
+    grad_rows = grad_out.flatten_outer_dims().rearrange("(p j) d -> p j d", j=PACK)
+    o_rows = o.flatten_outer_dims().rearrange("(p j) d -> p j d", j=PACK)
+    mu_rows = mu.flatten_outer_dims().rearrange("(p j) one -> p (j one)", j=PACK)
+    rstd_rows = rstd.flatten_outer_dims().rearrange("(p j) one -> p (j one)", j=PACK)
+
+    LAST = PACK - 1
+    QUARTER = N_TILE // 2
+
+    with tc.manual_schedule(), tc.tile_pool(name="keep", bufs=1) as keep, tc.tile_pool(
+        name="results", bufs=M_TILES * N_TILES
+    ) as results, tc.psum_pool(name="banks", bufs=8) as banks:
+        g_row = keep.tile([1, D], BF16)
+        rstd_sb = keep.tile([P, PACK], F32)
+        mu_sb = keep.tile([P, PACK], F32)
+        nc.sync.dma_start(out=g_row[:], in_=attn_norm_g.unsqueeze(0))
+        nc.scalar.dma_start(out=rstd_sb[:], in_=rstd_rows)
+        nc.scalar.dma_start(out=mu_sb[:], in_=mu_rows)
+
+        grad_sb = keep.tile([P, PACK, D], BF16)
+        h_halves = [keep.tile([P, PACK, DA // 2], BF16, name="h_half%d" % n) for n in range(2)]
+        o_sb = keep.tile([P, PACK, D], F32)
+        half_da = DA // 2
+        nc.sync.dma_start(out=grad_sb[:, 0, :], in_=grad_rows[:, 0, :])
+        nc.sync.dma_start(out=grad_sb[:, 1, :], in_=grad_rows[:, 1, :])
+        nc.sync.dma_start(out=o_sb[:, 0, :], in_=o_rows[:, 0, :])
+        nc.sync.dma_start(out=grad_sb[:, 2, :], in_=grad_rows[:, 2, :])
+        nc.sync.dma_start(out=h_halves[0][:], in_=h_rows[:, :, 0:half_da])
+        nc.sync.dma_start(out=grad_sb[:, 3, :], in_=grad_rows[:, 3, :])
+        for j in range(1, PACK):
+            nc.sync.dma_start(out=o_sb[:, j, :], in_=o_rows[:, j, :])
+        nc.sync.dma_start(out=h_halves[1][:], in_=h_rows[:, :, half_da:DA])
+
+        g_rows = keep.tile([P, D], BF16)
+        ones = keep.tile([P, P], BF16)
+        nc.vector.memset(g_rows[:], 0.0)
+        nc.vector.memset(ones[:], 1.0)
+        last_add = keep.tile([P, 2], F32)
+        nc.vector.memset(last_add[:], 0.0)
+        nc.vector.tensor_copy(out=g_rows[0:1, :], in_=g_row[:])
+        g_all = banks.tile([P, D], BF16, tag="bank")
+        for n in range(N_TILES):
+            cols = slice(n * N_TILE, (n + 1) * N_TILE)
+            nc.tensor.matmul(out=g_all[:, cols], lhsT=ones[:], rhs=g_rows[:, cols], start=True, stop=True)
+
+        a2_over_d = keep.tile([P, PACK], F32)
+        neg_mu = keep.tile([P, PACK], F32)
+        neg_mu_a2_over_d = keep.tile([P, PACK], F32)
+        last_mul = keep.tile([P, 2], F32)
+        nc.scalar.activation(out=a2_over_d[:], in_=rstd_sb[:], func=ACT.Square, scale=1.0 / 32.0)
+        nc.scalar.activation(
+            out=last_mul[:, 0:1], in_=rstd_sb[:, LAST : LAST + 1], func=ACT.Square, scale=1.0 / 32.0
+        )
+        nc.scalar.activation(out=neg_mu[:], in_=mu_sb[:], func=ACT.Identity, scale=-1.0)
+        for j in range(PACK):
+            nc.scalar.activation(
+                out=last_mul[:, 1:2] if j == LAST else neg_mu_a2_over_d[:, j : j + 1],
+                in_=a2_over_d[:, j : j + 1],
+                func=ACT.Identity,
+                scale=neg_mu[:, j : j + 1],
+            )
+
+        ga = keep.tile([P, PACK, D], F32)
+        ga_sum = keep.tile([P, PACK], F32)
+        for j in range(PACK):
+            nc.vector.scalar_tensor_tensor(
+                out=ga[:, j, :],
+                in0=grad_sb[:, j, :],
+                scalar=rstd_sb[:, j : j + 1],
+                in1=g_all[:],
+                op0=ALU.mult,
+                op1=ALU.mult,
+                accum_out=ga_sum[:, j : j + 1],
+            )
+
+        h_grouped = keep.tile([P, DA, PACK], BF16, align_bytes=64)
+        nc.scalar.copy(
+            out=h_grouped[:, 0:half_da, :].rearrange("p (c i) j -> p c j i", i=4),
+            in_=h_halves[0][:].rearrange("p j (c i) -> p c j i", i=4),
+        )
+
+        products = keep.tile([P, PACK, D], F32)
+        q_raw0 = keep.tile([P, 1], F32)
+        products0 = keep.tile([P, D], F32)
+        nc.gpsimd.tensor_tensor(out=products0[:], in0=o_sb[:, 0, :], in1=ga[:, 0, :], op=ALU.mult)
+        summed = keep.tile([P, D], F32)
+        nc.scalar.activation(out=summed[:], in_=products0[:], func=ACT.Identity, accum_out=q_raw0[:])
+
+        mean_ga = keep.tile([P, PACK], F32)
+        nc.scalar.activation(out=mean_ga[:], in_=ga_sum[:], func=ACT.Identity, scale=1.0 / D)
+        nc.scalar.activation(
+            out=last_add[:, 1:2], in_=ga_sum[:, LAST : LAST + 1], func=ACT.Identity, scale=1.0 / D
+        )
+
+        q_sum = keep.tile([P, PACK], F32)
+        q_sum0 = keep.tile([P, 1], F32)
+        slope = keep.tile([P, PACK], F32)
+        offset = keep.tile([P, PACK], F32)
+        last_line = keep.tile([P, 2], F32)
+        u_parts = [keep.tile([P, PACK, QUARTER], F32, name="u_part%d" % q) for q in range(4)]
+
+        def line_of(j):
+            if j == LAST:
+                return last_line[:, 0:1], last_line[:, 1:2]
+            return slope[:, j : j + 1], offset[:, j : j + 1]
+
+        def make_u(j, q):
+            scale_ap, bias_ap = line_of(j)
+            nc.scalar.activation(
+                out=u_parts[q][:, j, :],
+                in_=o_sb[:, j, q * QUARTER : (q + 1) * QUARTER],
+                func=ACT.Identity,
+                scale=scale_ap,
+                bias=bias_ap,
+            )
+
+        for j in range(PACK):
+            slot = slice(j, j + 1)
+            if j == 0:
+                nc.scalar.activation(
+                    out=q_sum0[:],
+                    in_=ga_sum[:, slot],
+                    func=ACT.Identity,
+                    scale=neg_mu[:, slot],
+                    bias=q_raw0[:],
+                )
+            else:
+                nc.vector.scalar_tensor_tensor(
+                    out=products[:, j, :],
+                    in0=o_sb[:, j, :],
+                    scalar=mu_sb[:, slot],
+                    in1=ga[:, j, :],
+                    op0=ALU.subtract,
+                    op1=ALU.mult,
+                    accum_out=q_sum[:, slot],
+                )
+            if j == LAST:
+                nc.vector.scalar_tensor_tensor(
+                    out=last_line[:],
+                    in0=last_mul[:],
+                    scalar=q_sum[:, slot],
+                    in1=last_add[:],
+                    op0=ALU.mult,
+                    op1=ALU.add,
+                )
+            else:
+                q_ap = q_sum0[:] if j == 0 else q_sum[:, slot]
+                nc.scalar.activation(out=slope[:, slot], in_=q_ap, func=ACT.Identity, scale=a2_over_d[:, slot])
+                nc.scalar.activation(
+                    out=offset[:, slot],
+                    in_=q_ap,
+                    func=ACT.Identity,
+                    scale=neg_mu_a2_over_d[:, slot],
+                    bias=mean_ga[:, slot],
+                )
+            make_u(j, 0)
+        for q in range(1, 4):
+            for j in range(PACK):
+                make_u(j, q)
+
+        h_codes = keep.tile([P, DA], U32, align_bytes=64)
+        h_scales = keep.tile([P, DA], U8, align_bytes=64)
+
+        def quantize_h(half):
+            cols = slice(half * half_da, (half + 1) * half_da)
+            nc.vector.quantize_mx(
+                out=h_codes[:, cols].bitcast(E4M3_X4),
+                scales=h_scales[:, cols],
+                in_=h_grouped[:, cols, :].rearrange("p c j -> p (c j)"),
+            )
+
+        do_grouped = keep.tile([P, D, PACK], BF16, align_bytes=64)
+        do_codes = keep.tile([P, D], U32, align_bytes=64)
+        do_scales = keep.tile([P, D], U8, align_bytes=64)
+
+        def make_do(q):
+            cols = slice(q * QUARTER, (q + 1) * QUARTER)
+            nc.vector.tensor_tensor(
+                out=do_grouped[:, cols, :].rearrange("p (c i) j -> p c j i", i=4),
+                in0=ga[:, :, cols].rearrange("p j (c i) -> p c j i", i=4),
+                in1=u_parts[q][:].rearrange("p j (c i) -> p c j i", i=4),
+                op=ALU.subtract,
+            )
+
+        def quantize_do(q):
+            cols = slice(q * QUARTER, (q + 1) * QUARTER)
+            nc.vector.quantize_mx(
+                out=do_codes[:, cols].bitcast(E5M2_X4),
+                scales=do_scales[:, cols],
+                in_=do_grouped[:, cols, :].rearrange("p d j -> p (d j)"),
+            )
+
+        def multiply(n, m, engine):
+            cols = slice(n * N_TILE, (n + 1) * N_TILE)
+            rows = slice(m * M_TILE, (m + 1) * M_TILE)
+            acc = banks.tile([P, N_TILE], F32, tag="bank")
+            nc.tensor.matmul_mx(
+                out=acc[:],
+                lhsT=h_codes[:, rows].bitcast(E4M3_X4),
+                lhsT_scale=h_scales[:, rows],
+                rhs=do_codes[:, cols].bitcast(E5M2_X4),
+                rhs_scale=do_scales[:, cols],
+                start=True,
+                stop=True,
+            )
+            result = results.tile([P, N_TILE], F32)
+            if engine == "scalar":
+                nc.scalar.copy(out=result[:], in_=acc[:])
+            else:
+                nc.vector.tensor_copy(out=result[:], in_=acc[:])
+            nc.sync.dma_start(out=out[rows, cols], in_=result[:])
+
+        quantize_h(0)
+        make_do(0)
+        warm_acc = banks.tile([P, N_TILE], F32, tag="bank")
+        for w in range(3):
+            nc.tensor.matmul(
+                out=warm_acc[:],
+                lhsT=ones[:],
+                rhs=do_grouped[:, 0 : N_TILE // PACK, :].rearrange("p d j -> p (d j)"),
+                start=True,
+                stop=True,
+            )
+        make_do(1)
+        quantize_do(0)
+        quantize_do(1)
+        for m in range(M_TILES // 2):
+            multiply(0, m, "scalar")
+        nc.vector.tensor_copy(
+            out=h_grouped[:, half_da:DA, :], in_=h_halves[1][:].rearrange("p j c -> p c j")
+        )
+        quantize_h(1)
+        for m in range(M_TILES // 2, M_TILES):
+            multiply(0, m, "scalar")
+        make_do(2)
+        make_do(3)
+        quantize_do(2)
+        quantize_do(3)
+        for m in range(M_TILES):
+            multiply(1, m, "scalar" if m % 2 == 1 else "vector")

@@ -34,8 +34,8 @@ def tile_dcadecoderblock_pb_v_kernel(
     mu_rows = mu.flatten_outer_dims().rearrange("(p j) one -> p (j one)", j=PACK)
     rstd_rows = rstd.flatten_outer_dims().rearrange("(p j) one -> p (j one)", j=PACK)
 
-    LAST = PACK - 1
     QUARTER = N_TILE // 2
+    G_COLS = 3 * D // 8
 
     with tc.manual_schedule(), tc.tile_pool(name="keep", bufs=1) as keep, tc.tile_pool(
         name="results", bufs=M_TILES * N_TILES
@@ -55,37 +55,33 @@ def tile_dcadecoderblock_pb_v_kernel(
         nc.sync.dma_start(out=grad_sb[:, 1, :], in_=grad_rows[:, 1, :])
         nc.sync.dma_start(out=o_sb[:, 0, :], in_=o_rows[:, 0, :])
         nc.sync.dma_start(out=grad_sb[:, 2, :], in_=grad_rows[:, 2, :])
-        nc.sync.dma_start(out=h_halves[0][:], in_=h_rows[:, :, 0:half_da])
+        nc.sync.dma_start(out=o_sb[:, 1, :], in_=o_rows[:, 1, :])
         nc.sync.dma_start(out=grad_sb[:, 3, :], in_=grad_rows[:, 3, :])
-        for j in range(1, PACK):
+        for j in range(2, PACK):
             nc.sync.dma_start(out=o_sb[:, j, :], in_=o_rows[:, j, :])
-        nc.sync.dma_start(out=h_halves[1][:], in_=h_rows[:, :, half_da:DA])
+        for n in range(2):
+            nc.sync.dma_start(out=h_halves[n][:], in_=h_rows[:, :, n * half_da : (n + 1) * half_da])
 
         g_rows = keep.tile([P, D], BF16)
         ones = keep.tile([P, P], BF16)
         nc.vector.memset(g_rows[:], 0.0)
         nc.vector.memset(ones[:], 1.0)
-        last_add = keep.tile([P, 2], F32)
-        nc.vector.memset(last_add[:], 0.0)
+        line_add = keep.tile([P, PACK, 2], F32)
+        nc.vector.memset(line_add[:], 0.0)
         nc.vector.tensor_copy(out=g_rows[0:1, :], in_=g_row[:])
         g_all = banks.tile([P, D], BF16, tag="bank")
         for n in range(N_TILES):
             cols = slice(n * N_TILE, (n + 1) * N_TILE)
             nc.tensor.matmul(out=g_all[:, cols], lhsT=ones[:], rhs=g_rows[:, cols], start=True, stop=True)
 
-        a2_over_d = keep.tile([P, PACK], F32)
+        line_mul = keep.tile([P, PACK, 2], F32)
         neg_mu = keep.tile([P, PACK], F32)
-        neg_mu_a2_over_d = keep.tile([P, PACK], F32)
-        last_mul = keep.tile([P, 2], F32)
-        nc.scalar.activation(out=a2_over_d[:], in_=rstd_sb[:], func=ACT.Square, scale=1.0 / 32.0)
-        nc.scalar.activation(
-            out=last_mul[:, 0:1], in_=rstd_sb[:, LAST : LAST + 1], func=ACT.Square, scale=1.0 / 32.0
-        )
+        nc.scalar.activation(out=line_mul[:, :, 0], in_=rstd_sb[:], func=ACT.Square, scale=1.0 / 32.0)
         nc.scalar.activation(out=neg_mu[:], in_=mu_sb[:], func=ACT.Identity, scale=-1.0)
         for j in range(PACK):
             nc.scalar.activation(
-                out=last_mul[:, 1:2] if j == LAST else neg_mu_a2_over_d[:, j : j + 1],
-                in_=a2_over_d[:, j : j + 1],
+                out=line_mul[:, j, 1:2],
+                in_=line_mul[:, j, 0:1],
                 func=ACT.Identity,
                 scale=neg_mu[:, j : j + 1],
             )
@@ -103,96 +99,103 @@ def tile_dcadecoderblock_pb_v_kernel(
                 accum_out=ga_sum[:, j : j + 1],
             )
 
-        h_grouped = keep.tile([P, DA, PACK], BF16, align_bytes=64)
-        nc.scalar.copy(
-            out=h_grouped[:, 0:half_da, :].rearrange("p (c i) j -> p c j i", i=4),
-            in_=h_halves[0][:].rearrange("p j (c i) -> p c j i", i=4),
-        )
-
         products = keep.tile([P, PACK, D], F32)
-        q_raw0 = keep.tile([P, 1], F32)
         products0 = keep.tile([P, D], F32)
+        products1 = keep.tile([P, G_COLS], F32)
         nc.gpsimd.tensor_tensor(out=products0[:], in0=o_sb[:, 0, :], in1=ga[:, 0, :], op=ALU.mult)
-        summed = keep.tile([P, D], F32)
-        nc.scalar.activation(out=summed[:], in_=products0[:], func=ACT.Identity, accum_out=q_raw0[:])
+        nc.gpsimd.tensor_tensor(out=products1[:], in0=o_sb[:, 1, 0:G_COLS], in1=ga[:, 1, 0:G_COLS], op=ALU.mult)
 
-        mean_ga = keep.tile([P, PACK], F32)
-        nc.scalar.activation(out=mean_ga[:], in_=ga_sum[:], func=ACT.Identity, scale=1.0 / D)
+        shift = keep.tile([P, 2], F32)
+        line_start = keep.tile([P, 2, 2], F32)
+        line1_part = keep.tile([P, 2], F32)
+        line0 = keep.tile([P, 2], F32)
+        line1 = keep.tile([P, 2], F32)
+        q_raw0 = keep.tile([P, 1], F32)
+        q_raw1 = keep.tile([P, 1], F32)
+        summed0 = keep.tile([P, D], F32)
+        summed1 = keep.tile([P, G_COLS], F32)
+
+        def add_line(out, j, factor, bias_of):
+            for i in range(2):
+                nc.scalar.activation(
+                    out=out[:, i : i + 1],
+                    in_=line_mul[:, j, i : i + 1],
+                    func=ACT.Identity,
+                    scale=factor,
+                    bias=bias_of[:, i : i + 1],
+                )
+
+        def start_line(j):
+            slot = slice(j, j + 1)
+            nc.scalar.activation(out=line_add[:, j, 1:2], in_=ga_sum[:, slot], func=ACT.Identity, scale=1.0 / D)
+            nc.scalar.activation(out=shift[:, slot], in_=ga_sum[:, slot], func=ACT.Identity, scale=neg_mu[:, slot])
+            add_line(line_start[:, j, :], j, shift[:, slot], line_add[:, j, :])
+
+        start_line(0)
+
+        start_line(1)
+        nc.scalar.activation(out=summed0[:], in_=products0[:], func=ACT.Identity, accum_out=q_raw0[:])
+        nc.scalar.activation(out=summed1[:], in_=products1[:], func=ACT.Identity, accum_out=q_raw1[:])
+        add_line(line0[:], 0, q_raw0[:], line_start[:, 0, :])
         nc.scalar.activation(
-            out=last_add[:, 1:2], in_=ga_sum[:, LAST : LAST + 1], func=ACT.Identity, scale=1.0 / D
+            out=line_add[:, 2:PACK, 1], in_=ga_sum[:, 2:PACK], func=ACT.Identity, scale=1.0 / D
         )
 
         q_sum = keep.tile([P, PACK], F32)
-        q_sum0 = keep.tile([P, 1], F32)
-        slope = keep.tile([P, PACK], F32)
-        offset = keep.tile([P, PACK], F32)
-        last_line = keep.tile([P, 2], F32)
+        line = keep.tile([P, PACK, 2], F32)
         u_parts = [keep.tile([P, PACK, QUARTER], F32, name="u_part%d" % q) for q in range(4)]
 
-        def line_of(j):
-            if j == LAST:
-                return last_line[:, 0:1], last_line[:, 1:2]
-            return slope[:, j : j + 1], offset[:, j : j + 1]
-
         def make_u(j, q):
-            scale_ap, bias_ap = line_of(j)
+            line_j = (line0[:], line1[:], line[:, 2, :], line[:, 3, :])[j]
             nc.scalar.activation(
                 out=u_parts[q][:, j, :],
                 in_=o_sb[:, j, q * QUARTER : (q + 1) * QUARTER],
                 func=ACT.Identity,
-                scale=scale_ap,
-                bias=bias_ap,
+                scale=line_j[:, 0:1],
+                bias=line_j[:, 1:2],
             )
 
-        for j in range(PACK):
-            slot = slice(j, j + 1)
-            if j == 0:
-                nc.scalar.activation(
-                    out=q_sum0[:],
-                    in_=ga_sum[:, slot],
-                    func=ACT.Identity,
-                    scale=neg_mu[:, slot],
-                    bias=q_raw0[:],
-                )
-            else:
-                nc.vector.scalar_tensor_tensor(
-                    out=products[:, j, :],
-                    in0=o_sb[:, j, :],
-                    scalar=mu_sb[:, slot],
-                    in1=ga[:, j, :],
-                    op0=ALU.subtract,
-                    op1=ALU.mult,
-                    accum_out=q_sum[:, slot],
-                )
-            if j == LAST:
-                nc.vector.scalar_tensor_tensor(
-                    out=last_line[:],
-                    in0=last_mul[:],
-                    scalar=q_sum[:, slot],
-                    in1=last_add[:],
-                    op0=ALU.mult,
-                    op1=ALU.add,
-                )
-            else:
-                q_ap = q_sum0[:] if j == 0 else q_sum[:, slot]
-                nc.scalar.activation(out=slope[:, slot], in_=q_ap, func=ACT.Identity, scale=a2_over_d[:, slot])
-                nc.scalar.activation(
-                    out=offset[:, slot],
-                    in_=q_ap,
-                    func=ACT.Identity,
-                    scale=neg_mu_a2_over_d[:, slot],
-                    bias=mean_ga[:, slot],
-                )
-            make_u(j, 0)
-        for q in range(1, 4):
-            for j in range(PACK):
-                make_u(j, q)
+        def sum_products(j):
+            first = G_COLS if j == 1 else 0
+            nc.vector.scalar_tensor_tensor(
+                out=products[:, j, first:D],
+                in0=o_sb[:, j, first:D],
+                scalar=1.0 if j == 1 else mu_sb[:, j : j + 1],
+                in1=ga[:, j, first:D],
+                op0=ALU.mult if j == 1 else ALU.subtract,
+                op1=ALU.mult,
+                accum_out=q_sum[:, j : j + 1],
+            )
+
+        def make_line(j):
+            nc.vector.scalar_tensor_tensor(
+                out=line[:, j, :],
+                in0=line_mul[:, j, :],
+                scalar=q_sum[:, j : j + 1],
+                in1=line_add[:, j, :],
+                op0=ALU.mult,
+                op1=ALU.add,
+            )
 
         h_codes = keep.tile([P, DA], U32, align_bytes=64)
         h_scales = keep.tile([P, DA], U8, align_bytes=64)
 
-        def quantize_h(half):
-            cols = slice(half * half_da, (half + 1) * half_da)
+        h_grouped = keep.tile([P, DA, PACK], BF16, align_bytes=64)
+
+        def lay_out_h(first, last):
+            nc.vector.tensor_copy(
+                out=h_grouped[:, first:last, :],
+                in_=h_halves[0][:, :, first:last].rearrange("p j c -> p c j"),
+            )
+
+        def lay_out_second_half():
+            nc.scalar.copy(
+                out=h_grouped[:, half_da:DA, :].rearrange("p (c i) j -> p c j i", i=4),
+                in_=h_halves[1][:].rearrange("p j (c i) -> p c j i", i=4),
+            )
+
+        def quantize_h(first, last):
+            cols = slice(first, last)
             nc.vector.quantize_mx(
                 out=h_codes[:, cols].bitcast(E4M3_X4),
                 scales=h_scales[:, cols],
@@ -240,27 +243,38 @@ def tile_dcadecoderblock_pb_v_kernel(
                 nc.vector.tensor_copy(out=result[:], in_=acc[:])
             nc.sync.dma_start(out=out[rows, cols], in_=result[:])
 
-        quantize_h(0)
+        sum_products(1)
+        add_line(line1_part[:], 1, q_sum[:, 1:2], line_start[:, 1, :])
+        add_line(line1[:], 1, q_raw1[:], line1_part[:])
+        for q in range(4):
+            make_u(0, q)
+        for q in range(2):
+            make_u(1, q)
+        sum_products(2)
+        sum_products(3)
+        make_line(2)
+        make_u(2, 0)
+        make_line(3)
+        make_u(3, 0)
+        lay_out_h(0, QUARTER)
+        quantize_h(0, QUARTER)
+        make_u(2, 1)
+        make_u(3, 1)
+        lay_out_second_half()
+        for j in range(1, PACK):
+            make_u(j, 2)
         make_do(0)
-        warm_acc = banks.tile([P, N_TILE], F32, tag="bank")
-        for w in range(3):
-            nc.tensor.matmul(
-                out=warm_acc[:],
-                lhsT=ones[:],
-                rhs=do_grouped[:, 0 : N_TILE // PACK, :].rearrange("p d j -> p (d j)"),
-                start=True,
-                stop=True,
-            )
         make_do(1)
         quantize_do(0)
         quantize_do(1)
-        for m in range(M_TILES // 2):
-            multiply(0, m, "scalar")
-        nc.vector.tensor_copy(
-            out=h_grouped[:, half_da:DA, :], in_=h_halves[1][:].rearrange("p j c -> p c j")
-        )
-        quantize_h(1)
-        for m in range(M_TILES // 2, M_TILES):
+        lay_out_h(QUARTER, half_da)
+        multiply(0, 0, "scalar")
+        for j in range(1, PACK):
+            make_u(j, 3)
+        quantize_h(half_da, DA)
+        quantize_h(QUARTER, half_da)
+        multiply(0, 1, "vector")
+        for m in range(2, M_TILES):
             multiply(0, m, "scalar")
         make_do(2)
         make_do(3)

@@ -55,8 +55,9 @@ def tile_dcadecoderblock_pb_v_kernel(
         nc.sync.dma_start(out=grad_sb[:, 1, :], in_=grad_rows[:, 1, :])
         nc.sync.dma_start(out=o_sb[:, 0, :], in_=o_rows[:, 0, :])
         nc.sync.dma_start(out=grad_sb[:, 2, :], in_=grad_rows[:, 2, :])
-        nc.sync.dma_start(out=o_sb[:, 1, :], in_=o_rows[:, 1, :])
+        nc.sync.dma_start(out=o_sb[:, 1, 0:N_TILE], in_=o_rows[:, 1, 0:N_TILE])
         nc.sync.dma_start(out=grad_sb[:, 3, :], in_=grad_rows[:, 3, :])
+        nc.sync.dma_start(out=o_sb[:, 1, N_TILE:D], in_=o_rows[:, 1, N_TILE:D])
         for j in range(2, PACK):
             nc.sync.dma_start(out=o_sb[:, j, :], in_=o_rows[:, j, :])
         for n in range(2):
@@ -66,13 +67,21 @@ def tile_dcadecoderblock_pb_v_kernel(
         ones = keep.tile([P, P], BF16)
         nc.vector.memset(g_rows[:], 0.0)
         nc.vector.memset(ones[:], 1.0)
+        warm_ones = keep.tile([P, P], F32)
+        nc.vector.memset(warm_ones[:], 1.0)
         line_add = keep.tile([P, PACK, 2], F32)
         nc.vector.memset(line_add[:], 0.0)
         nc.vector.tensor_copy(out=g_rows[0:1, :], in_=g_row[:])
-        g_all = banks.tile([P, D], BF16, tag="bank")
-        for n in range(N_TILES):
+        def spread_g(g_bank, n):
             cols = slice(n * N_TILE, (n + 1) * N_TILE)
-            nc.tensor.matmul(out=g_all[:, cols], lhsT=ones[:], rhs=g_rows[:, cols], start=True, stop=True)
+            nc.tensor.matmul(out=g_bank, lhsT=ones[:], rhs=g_rows[:, cols], start=True, stop=True)
+
+        g_halves = [banks.tile([P, N_TILE], BF16, tag="bank", name="g_half%d" % n) for n in range(2)]
+        g_all = banks.tile([P, D], BF16, tag="bank")
+        for n in range(2):
+            spread_g(g_halves[n][:], n)
+        for n in range(2):
+            spread_g(g_all[:, n * N_TILE : (n + 1) * N_TILE], n)
 
         line_mul = keep.tile([P, PACK, 2], F32)
         neg_mu = keep.tile([P, PACK], F32)
@@ -88,16 +97,24 @@ def tile_dcadecoderblock_pb_v_kernel(
 
         ga = keep.tile([P, PACK, D], F32)
         ga_sum = keep.tile([P, PACK], F32)
-        for j in range(PACK):
+        ga_part = keep.tile([P, 2, 2], F32)
+
+        def make_ga(j, cols, g_ap, sum_ap):
             nc.vector.scalar_tensor_tensor(
-                out=ga[:, j, :],
-                in0=grad_sb[:, j, :],
+                out=ga[:, j, cols],
+                in0=grad_sb[:, j, cols],
                 scalar=rstd_sb[:, j : j + 1],
-                in1=g_all[:],
+                in1=g_ap,
                 op0=ALU.mult,
                 op1=ALU.mult,
-                accum_out=ga_sum[:, j : j + 1],
+                accum_out=sum_ap,
             )
+
+        for j in range(2):
+            for n in range(2):
+                make_ga(j, slice(n * N_TILE, (n + 1) * N_TILE), g_halves[n][:], ga_part[:, j, n : n + 1])
+        for j in range(2, PACK):
+            make_ga(j, slice(0, D), g_all[:], ga_sum[:, j : j + 1])
 
         products = keep.tile([P, PACK, D], F32)
         products0 = keep.tile([P, D], F32)
@@ -127,6 +144,9 @@ def tile_dcadecoderblock_pb_v_kernel(
 
         def start_line(j):
             slot = slice(j, j + 1)
+            nc.scalar.activation(
+                out=ga_sum[:, slot], in_=ga_part[:, j, 0:1], func=ACT.Identity, bias=ga_part[:, j, 1:2]
+            )
             nc.scalar.activation(out=line_add[:, j, 1:2], in_=ga_sum[:, slot], func=ACT.Identity, scale=1.0 / D)
             nc.scalar.activation(out=shift[:, slot], in_=ga_sum[:, slot], func=ACT.Identity, scale=neg_mu[:, slot])
             add_line(line_start[:, j, :], j, shift[:, slot], line_add[:, j, :])
@@ -246,10 +266,11 @@ def tile_dcadecoderblock_pb_v_kernel(
         sum_products(1)
         add_line(line1_part[:], 1, q_sum[:, 1:2], line_start[:, 1, :])
         add_line(line1[:], 1, q_raw1[:], line1_part[:])
-        for q in range(4):
-            make_u(0, q)
         for q in range(2):
-            make_u(1, q)
+            for j in range(2):
+                make_u(j, q)
+        for q in range(2, 4):
+            make_u(0, q)
         sum_products(2)
         sum_products(3)
         make_line(2)
@@ -260,6 +281,11 @@ def tile_dcadecoderblock_pb_v_kernel(
         quantize_h(0, QUARTER)
         make_u(2, 1)
         make_u(3, 1)
+        warm_acc = banks.tile([P, N_TILE], F32, tag="bank")
+        for j in range(2, PACK):
+            nc.tensor.matmul(
+                out=warm_acc[:, 0:QUARTER], lhsT=warm_ones[:], rhs=u_parts[0][:, j, :], start=True, stop=True
+            )
         lay_out_second_half()
         for j in range(1, PACK):
             make_u(j, 2)

@@ -71,7 +71,9 @@ def tile_dcadecoderblock_pb_v_kernel(
         nc.vector.memset(warm_ones[:], 1.0)
         line_add = keep.tile([P, PACK, 2], F32)
         nc.vector.memset(line_add[:], 0.0)
-        nc.vector.tensor_copy(out=g_rows[0:1, :], in_=g_row[:])
+        for n in range(2):
+            cols = slice(n * N_TILE, (n + 1) * N_TILE)
+            nc.vector.tensor_copy(out=g_rows[0:1, cols], in_=g_row[:, cols])
         def spread_g(g_bank, n):
             cols = slice(n * N_TILE, (n + 1) * N_TILE)
             nc.tensor.matmul(out=g_bank, lhsT=ones[:], rhs=g_rows[:, cols], start=True, stop=True)
@@ -202,17 +204,18 @@ def tile_dcadecoderblock_pb_v_kernel(
 
         h_grouped = keep.tile([P, DA, PACK], BF16, align_bytes=64)
 
-        def lay_out_h(first, last):
-            nc.vector.tensor_copy(
-                out=h_grouped[:, first:last, :],
-                in_=h_halves[0][:, :, first:last].rearrange("p j c -> p c j"),
-            )
-
-        def lay_out_second_half():
-            nc.scalar.copy(
-                out=h_grouped[:, half_da:DA, :].rearrange("p (c i) j -> p c j i", i=4),
-                in_=h_halves[1][:].rearrange("p j (c i) -> p c j i", i=4),
-            )
+        def lay_out_h(first, last, engine):
+            half = first // half_da
+            cols = slice(first - half * half_da, last - half * half_da)
+            if engine == "vector":
+                nc.vector.tensor_copy(
+                    out=h_grouped[:, first:last, :], in_=h_halves[half][:, :, cols].rearrange("p j c -> p c j")
+                )
+            else:
+                nc.scalar.copy(
+                    out=h_grouped[:, first:last, :].rearrange("p (c i) j -> p c j i", i=4),
+                    in_=h_halves[half][:, :, cols].rearrange("p j (c i) -> p c j i", i=4),
+                )
 
         def quantize_h(first, last):
             cols = slice(first, last)
@@ -275,9 +278,10 @@ def tile_dcadecoderblock_pb_v_kernel(
         sum_products(3)
         make_line(2)
         make_u(2, 0)
+        lay_out_h(0, M_TILE, "vector")
         make_line(3)
         make_u(3, 0)
-        lay_out_h(0, QUARTER)
+        lay_out_h(M_TILE, QUARTER, "vector")
         quantize_h(0, QUARTER)
         make_u(2, 1)
         make_u(3, 1)
@@ -286,21 +290,24 @@ def tile_dcadecoderblock_pb_v_kernel(
             nc.tensor.matmul(
                 out=warm_acc[:, 0:QUARTER], lhsT=warm_ones[:], rhs=u_parts[0][:, j, :], start=True, stop=True
             )
-        lay_out_second_half()
-        for j in range(1, PACK):
-            make_u(j, 2)
+        lay_out_h(half_da, half_da + QUARTER, "scalar")
+        for q in range(2, 4):
+            for j in range(1, PACK):
+                make_u(j, q)
         make_do(0)
         make_do(1)
         quantize_do(0)
         quantize_do(1)
-        lay_out_h(QUARTER, half_da)
-        multiply(0, 0, "scalar")
-        for j in range(1, PACK):
-            make_u(j, 3)
+        for m in range(2):
+            multiply(0, m, "scalar")
+        for m in range(2, M_TILES // 2):
+            lay_out_h(m * M_TILE, (m + 1) * M_TILE, "vector")
+        for m in range(2, M_TILES // 2):
+            quantize_h(m * M_TILE, (m + 1) * M_TILE)
+            multiply(0, m, "scalar")
+        lay_out_h(half_da + QUARTER, DA, "vector")
         quantize_h(half_da, DA)
-        quantize_h(QUARTER, half_da)
-        multiply(0, 1, "vector")
-        for m in range(2, M_TILES):
+        for m in range(M_TILES // 2, M_TILES):
             multiply(0, m, "scalar")
         make_do(2)
         make_do(3)

@@ -207,15 +207,12 @@ def tile_dcadecoderblock_pb_v_kernel(
         def lay_out_h(first, last, engine):
             half = first // half_da
             cols = slice(first - half * half_da, last - half * half_da)
+            grouped = h_grouped[:, first:last, :].rearrange("p (c i) j -> p c j i", i=4)
+            plain = h_halves[half][:, :, cols].rearrange("p j (c i) -> p c j i", i=4)
             if engine == "vector":
-                nc.vector.tensor_copy(
-                    out=h_grouped[:, first:last, :], in_=h_halves[half][:, :, cols].rearrange("p j c -> p c j")
-                )
+                nc.vector.tensor_copy(out=grouped, in_=plain)
             else:
-                nc.scalar.copy(
-                    out=h_grouped[:, first:last, :].rearrange("p (c i) j -> p c j i", i=4),
-                    in_=h_halves[half][:, :, cols].rearrange("p j (c i) -> p c j i", i=4),
-                )
+                nc.scalar.copy(out=grouped, in_=plain)
 
         def quantize_h(first, last):
             cols = slice(first, last)

@@ -35,7 +35,7 @@ def tile_dcadecoderblock_pb_v_kernel(
     rstd_rows = rstd.flatten_outer_dims().rearrange("(p j) one -> p (j one)", j=PACK)
 
     QUARTER = N_TILE // 2
-    G_COLS = 3 * D // 8
+    G_COLS = D // 4
 
     with tc.manual_schedule(), tc.tile_pool(name="keep", bufs=1) as keep, tc.tile_pool(
         name="results", bufs=M_TILES * N_TILES

@@ -35,7 +35,7 @@ def tile_dcadecoderblock_pb_v_kernel(
     rstd_rows = rstd.flatten_outer_dims().rearrange("(p j) one -> p (j one)", j=PACK)
 
     QUARTER = N_TILE // 2
-    G_COLS = D // 4
+    G_COLS = D // 2
 
     with tc.manual_schedule(), tc.tile_pool(name="keep", bufs=1) as keep, tc.tile_pool(
         name="results", bufs=M_TILES * N_TILES
@@ -52,8 +52,9 @@ def tile_dcadecoderblock_pb_v_kernel(
         o_sb = keep.tile([P, PACK, D], F32)
         half_da = DA // 2
         nc.sync.dma_start(out=grad_sb[:, 0, :], in_=grad_rows[:, 0, :])
+        nc.sync.dma_start(out=o_sb[:, 0, 0:N_TILE], in_=o_rows[:, 0, 0:N_TILE])
         nc.sync.dma_start(out=grad_sb[:, 1, :], in_=grad_rows[:, 1, :])
-        nc.sync.dma_start(out=o_sb[:, 0, :], in_=o_rows[:, 0, :])
+        nc.sync.dma_start(out=o_sb[:, 0, N_TILE:D], in_=o_rows[:, 0, N_TILE:D])
         nc.sync.dma_start(out=grad_sb[:, 2, :], in_=grad_rows[:, 2, :])
         nc.sync.dma_start(out=o_sb[:, 1, 0:N_TILE], in_=o_rows[:, 1, 0:N_TILE])
         nc.sync.dma_start(out=grad_sb[:, 3, :], in_=grad_rows[:, 3, :])
@@ -121,7 +122,9 @@ def tile_dcadecoderblock_pb_v_kernel(
         products = keep.tile([P, PACK, D], F32)
         products0 = keep.tile([P, D], F32)
         products1 = keep.tile([P, G_COLS], F32)
-        nc.gpsimd.tensor_tensor(out=products0[:], in0=o_sb[:, 0, :], in1=ga[:, 0, :], op=ALU.mult)
+        for n in range(2):
+            cols = slice(n * N_TILE, (n + 1) * N_TILE)
+            nc.gpsimd.tensor_tensor(out=products0[:, cols], in0=o_sb[:, 0, cols], in1=ga[:, 0, cols], op=ALU.mult)
         nc.gpsimd.tensor_tensor(out=products1[:], in0=o_sb[:, 1, 0:G_COLS], in1=ga[:, 1, 0:G_COLS], op=ALU.mult)
 
         shift = keep.tile([P, 2], F32)
@@ -275,11 +278,12 @@ def tile_dcadecoderblock_pb_v_kernel(
         sum_products(3)
         make_line(2)
         make_u(2, 0)
-        lay_out_h(0, M_TILE, "vector")
         make_line(3)
         make_u(3, 0)
-        lay_out_h(M_TILE, QUARTER, "vector")
-        quantize_h(0, QUARTER)
+        for m in range(2):
+            lay_out_h(m * M_TILE, (m + 1) * M_TILE, "vector")
+        for m in range(2):
+            quantize_h(m * M_TILE, (m + 1) * M_TILE)
         make_u(2, 1)
         make_u(3, 1)
         warm_acc = banks.tile([P, N_TILE], F32, tag="bank")
@@ -287,10 +291,11 @@ def tile_dcadecoderblock_pb_v_kernel(
             nc.tensor.matmul(
                 out=warm_acc[:, 0:QUARTER], lhsT=warm_ones[:], rhs=u_parts[0][:, j, :], start=True, stop=True
             )
+        for j in range(1, PACK):
+            make_u(j, 2)
         lay_out_h(half_da, half_da + QUARTER, "scalar")
-        for q in range(2, 4):
-            for j in range(1, PACK):
-                make_u(j, q)
+        for j in range(1, PACK):
+            make_u(j, 3)
         make_do(0)
         make_do(1)
         quantize_do(0)

@@ -267,47 +267,55 @@ def tile_dcadecoderblock_pb_v_kernel(
             nc.sync.dma_start(out=out[rows, cols], in_=result[:])
 
         sum_products(1)
+        make_u(0, 0)
+        make_u(0, 1)
         add_line(line1_part[:], 1, q_sum[:, 1:2], line_start[:, 1, :])
+        make_u(0, 2)
         add_line(line1[:], 1, q_raw1[:], line1_part[:])
-        for q in range(2):
-            for j in range(2):
-                make_u(j, q)
-        for q in range(2, 4):
-            make_u(0, q)
+        make_u(0, 3)
+        for q in range(4):
+            make_u(1, q)
         sum_products(2)
         sum_products(3)
         make_line(2)
         make_u(2, 0)
         make_line(3)
-        make_u(3, 0)
-        for m in range(2):
-            lay_out_h(m * M_TILE, (m + 1) * M_TILE, "vector")
-        for m in range(2):
-            quantize_h(m * M_TILE, (m + 1) * M_TILE)
+        lay_out_h(0, M_TILE, "vector")
+        nc.vector.tensor_scalar(
+            out=u_parts[0][:, 3, :],
+            in0=o_sb[:, 3, 0:QUARTER],
+            scalar1=line[:, 3, 0:1],
+            scalar2=line[:, 3, 1:2],
+            op0=ALU.mult,
+            op1=ALU.add,
+        )
+        quantize_h(0, M_TILE)
         make_u(2, 1)
         make_u(3, 1)
         warm_acc = banks.tile([P, N_TILE], F32, tag="bank")
-        for j in range(2, PACK):
+        for q in range(2):
             nc.tensor.matmul(
-                out=warm_acc[:, 0:QUARTER], lhsT=warm_ones[:], rhs=u_parts[0][:, j, :], start=True, stop=True
+                out=warm_acc[:, 0:QUARTER], lhsT=warm_ones[:], rhs=u_parts[q][:, 2, :], start=True, stop=True
             )
-        for j in range(1, PACK):
-            make_u(j, 2)
+        for q in range(2, 4):
+            for j in range(2, PACK):
+                make_u(j, q)
+        lay_out_h(M_TILE, QUARTER, "scalar")
         lay_out_h(half_da, half_da + QUARTER, "scalar")
-        for j in range(1, PACK):
-            make_u(j, 3)
         make_do(0)
         make_do(1)
         quantize_do(0)
         quantize_do(1)
+        quantize_h(M_TILE, QUARTER)
         for m in range(2):
             multiply(0, m, "scalar")
         for m in range(2, M_TILES // 2):
             lay_out_h(m * M_TILE, (m + 1) * M_TILE, "vector")
-        for m in range(2, M_TILES // 2):
-            quantize_h(m * M_TILE, (m + 1) * M_TILE)
-            multiply(0, m, "scalar")
+        quantize_h(2 * M_TILE, 3 * M_TILE)
+        multiply(0, 2, "scalar")
         lay_out_h(half_da + QUARTER, DA, "vector")
+        quantize_h(3 * M_TILE, half_da)
+        multiply(0, 3, "scalar")
         quantize_h(half_da, DA)
         for m in range(M_TILES // 2, M_TILES):
             multiply(0, m, "scalar")

import concourse.mybir as mybir

F32 = mybir.dt.float32
BF16 = mybir.dt.bfloat16
U32 = mybir.dt.uint32
U8 = mybir.dt.uint8
E4M3_X4 = mybir.dt.float8_e4m3fn_x4
E5M2_X4 = mybir.dt.float8_e5m2_x4
ALU = mybir.AluOpType
ACT = mybir.ActivationFunctionType

P = 128
PACK = 4
TOKENS = P * PACK
DA = 1024
D = 1024
M_TILE = 128
N_TILE = 512
M_TILES = DA // M_TILE
N_TILES = D // N_TILE

FLOPS = 2 * TOKENS * DA * D
BYTES = 2 * TOKENS * DA + 2 * TOKENS * D + 4 * TOKENS * D + 2 * D + 8 * TOKENS + 4 * DA * D


def tile_dcadecoderblock_pb_v_kernel(
    tc, h_attn, x, attn_out_W, attn_out_b, attn_norm_g, attn_norm_b, o, mu, rstd, grad_out, out
):
    nc = tc.nc

    h_rows = h_attn.flatten_outer_dims().rearrange("(p j) c -> p j c", j=PACK)
    grad_rows = grad_out.flatten_outer_dims().rearrange("(p j) d -> p j d", j=PACK)
    o_rows = o.flatten_outer_dims().rearrange("(p j) d -> p j d", j=PACK)
    mu_rows = mu.flatten_outer_dims().rearrange("(p j) one -> p (j one)", j=PACK)
    rstd_rows = rstd.flatten_outer_dims().rearrange("(p j) one -> p (j one)", j=PACK)

    QUARTER = N_TILE // 2
    G_COLS = D // 2

    with tc.manual_schedule(), tc.tile_pool(name="keep", bufs=1) as keep, tc.tile_pool(
        name="results", bufs=M_TILES * N_TILES
    ) as results, tc.psum_pool(name="banks", bufs=8) as banks:
        g_row = keep.tile([1, D], BF16)
        rstd_sb = keep.tile([P, PACK], F32)
        mu_sb = keep.tile([P, PACK], F32)
        nc.sync.dma_start(out=g_row[:], in_=attn_norm_g.unsqueeze(0))
        nc.scalar.dma_start(out=rstd_sb[:], in_=rstd_rows)
        nc.scalar.dma_start(out=mu_sb[:], in_=mu_rows)

        grad_sb = keep.tile([P, PACK, D], BF16)
        h_halves = [keep.tile([P, PACK, DA // 2], BF16, name="h_half%d" % n) for n in range(2)]
        o_sb = keep.tile([P, PACK, D], F32)
        half_da = DA // 2
        nc.sync.dma_start(out=grad_sb[:, 0, :], in_=grad_rows[:, 0, :])
        nc.sync.dma_start(out=o_sb[:, 0, 0:N_TILE], in_=o_rows[:, 0, 0:N_TILE])
        nc.sync.dma_start(out=grad_sb[:, 1, :], in_=grad_rows[:, 1, :])
        nc.sync.dma_start(out=o_sb[:, 0, N_TILE:D], in_=o_rows[:, 0, N_TILE:D])
        nc.sync.dma_start(out=grad_sb[:, 2, :], in_=grad_rows[:, 2, :])
        nc.sync.dma_start(out=o_sb[:, 1, 0:N_TILE], in_=o_rows[:, 1, 0:N_TILE])
        nc.sync.dma_start(out=grad_sb[:, 3, :], in_=grad_rows[:, 3, :])
        nc.sync.dma_start(out=o_sb[:, 1, N_TILE:D], in_=o_rows[:, 1, N_TILE:D])
        for j in range(2, PACK):
            nc.sync.dma_start(out=o_sb[:, j, :], in_=o_rows[:, j, :])
        for n in range(2):
            nc.sync.dma_start(out=h_halves[n][:], in_=h_rows[:, :, n * half_da : (n + 1) * half_da])

        g_rows = keep.tile([P, D], BF16)
        ones = keep.tile([P, P], BF16)
        nc.vector.memset(g_rows[:], 0.0)
        nc.vector.memset(ones[:], 1.0)
        warm_ones = keep.tile([P, P], F32)
        nc.vector.memset(warm_ones[:], 1.0)
        line_add = keep.tile([P, PACK, 2], F32)
        nc.vector.memset(line_add[:], 0.0)
        for n in range(2):
            cols = slice(n * N_TILE, (n + 1) * N_TILE)
            nc.vector.tensor_copy(out=g_rows[0:1, cols], in_=g_row[:, cols])
        def spread_g(g_bank, n):
            cols = slice(n * N_TILE, (n + 1) * N_TILE)
            nc.tensor.matmul(out=g_bank, lhsT=ones[:], rhs=g_rows[:, cols], start=True, stop=True)

        g_halves = [banks.tile([P, N_TILE], BF16, tag="bank", name="g_half%d" % n) for n in range(2)]
        g_all = banks.tile([P, D], BF16, tag="bank")
        for n in range(2):
            spread_g(g_halves[n][:], n)
        for n in range(2):
            spread_g(g_all[:, n * N_TILE : (n + 1) * N_TILE], n)

        line_mul = keep.tile([P, PACK, 2], F32)
        neg_mu = keep.tile([P, PACK], F32)
        nc.scalar.activation(out=line_mul[:, :, 0], in_=rstd_sb[:], func=ACT.Square, scale=1.0 / 32.0)
        nc.scalar.activation(out=neg_mu[:], in_=mu_sb[:], func=ACT.Identity, scale=-1.0)
        for j in range(PACK):
            nc.scalar.activation(
                out=line_mul[:, j, 1:2],
                in_=line_mul[:, j, 0:1],
                func=ACT.Identity,
                scale=neg_mu[:, j : j + 1],
            )

        ga = keep.tile([P, PACK, D], F32)
        ga_sum = keep.tile([P, PACK], F32)
        ga_part = keep.tile([P, 2, 2], F32)

        def make_ga(j, cols, g_ap, sum_ap):
            nc.vector.scalar_tensor_tensor(
                out=ga[:, j, cols],
                in0=grad_sb[:, j, cols],
                scalar=rstd_sb[:, j : j + 1],
                in1=g_ap,
                op0=ALU.mult,
                op1=ALU.mult,
                accum_out=sum_ap,
            )

        for j in range(2):
            for n in range(2):
                make_ga(j, slice(n * N_TILE, (n + 1) * N_TILE), g_halves[n][:], ga_part[:, j, n : n + 1])
        for j in range(2, PACK):
            make_ga(j, slice(0, D), g_all[:], ga_sum[:, j : j + 1])

        products = keep.tile([P, PACK, D], F32)
        products0 = keep.tile([P, D], F32)
        products1 = keep.tile([P, G_COLS], F32)
        for n in range(2):
            cols = slice(n * N_TILE, (n + 1) * N_TILE)
            nc.gpsimd.tensor_tensor(out=products0[:, cols], in0=o_sb[:, 0, cols], in1=ga[:, 0, cols], op=ALU.mult)
        nc.gpsimd.tensor_tensor(out=products1[:], in0=o_sb[:, 1, 0:G_COLS], in1=ga[:, 1, 0:G_COLS], op=ALU.mult)

        shift = keep.tile([P, 2], F32)
        line_start = keep.tile([P, 2, 2], F32)
        line1_part = keep.tile([P, 2], F32)
        line0 = keep.tile([P, 2], F32)
        line1 = keep.tile([P, 2], F32)
        q_raw0 = keep.tile([P, 1], F32)
        q_raw1 = keep.tile([P, 1], F32)
        summed0 = keep.tile([P, D], F32)
        summed1 = keep.tile([P, G_COLS], F32)

        def add_line(out, j, factor, bias_of):
            for i in range(2):
                nc.scalar.activation(
                    out=out[:, i : i + 1],
                    in_=line_mul[:, j, i : i + 1],
                    func=ACT.Identity,
                    scale=factor,
                    bias=bias_of[:, i : i + 1],
                )

        def start_line(j):
            slot = slice(j, j + 1)
            nc.scalar.activation(
                out=ga_sum[:, slot], in_=ga_part[:, j, 0:1], func=ACT.Identity, bias=ga_part[:, j, 1:2]
            )
            nc.scalar.activation(out=line_add[:, j, 1:2], in_=ga_sum[:, slot], func=ACT.Identity, scale=1.0 / D)
            nc.scalar.activation(out=shift[:, slot], in_=ga_sum[:, slot], func=ACT.Identity, scale=neg_mu[:, slot])
            add_line(line_start[:, j, :], j, shift[:, slot], line_add[:, j, :])

        start_line(0)

        start_line(1)
        nc.scalar.activation(out=summed0[:], in_=products0[:], func=ACT.Identity, accum_out=q_raw0[:])
        nc.scalar.activation(out=summed1[:], in_=products1[:], func=ACT.Identity, accum_out=q_raw1[:])
        add_line(line0[:], 0, q_raw0[:], line_start[:, 0, :])
        nc.scalar.activation(
            out=line_add[:, 2:PACK, 1], in_=ga_sum[:, 2:PACK], func=ACT.Identity, scale=1.0 / D
        )

        q_sum = keep.tile([P, PACK], F32)
        line = keep.tile([P, PACK, 2], F32)
        u_parts = [keep.tile([P, PACK, QUARTER], F32, name="u_part%d" % q) for q in range(4)]

        def make_u(j, q):
            line_j = (line0[:], line1[:], line[:, 2, :], line[:, 3, :])[j]
            nc.scalar.activation(
                out=u_parts[q][:, j, :],
                in_=o_sb[:, j, q * QUARTER : (q + 1) * QUARTER],
                func=ACT.Identity,
                scale=line_j[:, 0:1],
                bias=line_j[:, 1:2],
            )

        def sum_products(j):
            first = G_COLS if j == 1 else 0
            nc.vector.scalar_tensor_tensor(
                out=products[:, j, first:D],
                in0=o_sb[:, j, first:D],
                scalar=1.0 if j == 1 else mu_sb[:, j : j + 1],
                in1=ga[:, j, first:D],
                op0=ALU.mult if j == 1 else ALU.subtract,
                op1=ALU.mult,
                accum_out=q_sum[:, j : j + 1],
            )

        def make_line(j):
            nc.vector.scalar_tensor_tensor(
                out=line[:, j, :],
                in0=line_mul[:, j, :],
                scalar=q_sum[:, j : j + 1],
                in1=line_add[:, j, :],
                op0=ALU.mult,
                op1=ALU.add,
            )

        h_codes = keep.tile([P, DA], U32, align_bytes=64)
        h_scales = keep.tile([P, DA], U8, align_bytes=64)

        h_grouped = keep.tile([P, DA, PACK], BF16, align_bytes=64)

        def lay_out_h(first, last, engine):
            half = first // half_da
            cols = slice(first - half * half_da, last - half * half_da)
            grouped = h_grouped[:, first:last, :].rearrange("p (c i) j -> p c j i", i=4)
            plain = h_halves[half][:, :, cols].rearrange("p j (c i) -> p c j i", i=4)
            if engine == "vector":
                nc.vector.tensor_copy(out=grouped, in_=plain)
            else:
                nc.scalar.copy(out=grouped, in_=plain)

        def quantize_h(first, last):
            cols = slice(first, last)
            nc.vector.quantize_mx(
                out=h_codes[:, cols].bitcast(E4M3_X4),
                scales=h_scales[:, cols],
                in_=h_grouped[:, cols, :].rearrange("p c j -> p (c j)"),
            )

        do_grouped = keep.tile([P, D, PACK], BF16, align_bytes=64)
        do_codes = keep.tile([P, D], U32, align_bytes=64)
        do_scales = keep.tile([P, D], U8, align_bytes=64)

        def make_do(q):
            cols = slice(q * QUARTER, (q + 1) * QUARTER)
            nc.vector.tensor_tensor(
                out=do_grouped[:, cols, :].rearrange("p (c i) j -> p c j i", i=4),
                in0=ga[:, :, cols].rearrange("p j (c i) -> p c j i", i=4),
                in1=u_parts[q][:].rearrange("p j (c i) -> p c j i", i=4),
                op=ALU.subtract,
            )

        def quantize_do(q):
            cols = slice(q * QUARTER, (q + 1) * QUARTER)
            nc.vector.quantize_mx(
                out=do_codes[:, cols].bitcast(E5M2_X4),
                scales=do_scales[:, cols],
                in_=do_grouped[:, cols, :].rearrange("p d j -> p (d j)"),
            )

        def multiply(n, m, engine):
            cols = slice(n * N_TILE, (n + 1) * N_TILE)
            rows = slice(m * M_TILE, (m + 1) * M_TILE)
            acc = banks.tile([P, N_TILE], F32, tag="bank")
            nc.tensor.matmul_mx(
                out=acc[:],
                lhsT=h_codes[:, rows].bitcast(E4M3_X4),
                lhsT_scale=h_scales[:, rows],
                rhs=do_codes[:, cols].bitcast(E5M2_X4),
                rhs_scale=do_scales[:, cols],
                start=True,
                stop=True,
            )
            result = results.tile([P, N_TILE], F32)
            if engine == "scalar":
                nc.scalar.copy(out=result[:], in_=acc[:])
            else:
                nc.vector.tensor_copy(out=result[:], in_=acc[:])
            nc.sync.dma_start(out=out[rows, cols], in_=result[:])

        sum_products(1)
        make_u(0, 0)
        make_u(0, 1)
        add_line(line1_part[:], 1, q_sum[:, 1:2], line_start[:, 1, :])
        make_u(0, 2)
        add_line(line1[:], 1, q_raw1[:], line1_part[:])
        make_u(0, 3)
        for q in range(4):
            make_u(1, q)
        sum_products(2)
        sum_products(3)
        make_line(2)
        make_u(2, 0)
        make_line(3)
        lay_out_h(0, M_TILE, "vector")
        nc.vector.tensor_scalar(
            out=u_parts[0][:, 3, :],
            in0=o_sb[:, 3, 0:QUARTER],
            scalar1=line[:, 3, 0:1],
            scalar2=line[:, 3, 1:2],
            op0=ALU.mult,
            op1=ALU.add,
        )
        quantize_h(0, M_TILE)
        make_u(2, 1)
        make_u(3, 1)
        warm_acc = banks.tile([P, N_TILE], F32, tag="bank")
        for q in range(2):
            nc.tensor.matmul(
                out=warm_acc[:, 0:QUARTER], lhsT=warm_ones[:], rhs=u_parts[q][:, 2, :], start=True, stop=True
            )
        for q in range(2, 4):
            for j in range(2, PACK):
                make_u(j, q)
        lay_out_h(M_TILE, QUARTER, "scalar")
        lay_out_h(half_da, half_da + QUARTER, "scalar")
        make_do(0)
        make_do(1)
        quantize_do(0)
        quantize_do(1)
        quantize_h(M_TILE, QUARTER)
        for m in range(2):
            multiply(0, m, "scalar")
        for m in range(2, M_TILES // 2):
            lay_out_h(m * M_TILE, (m + 1) * M_TILE, "vector")
        quantize_h(2 * M_TILE, 3 * M_TILE)
        multiply(0, 2, "scalar")
        lay_out_h(half_da + QUARTER, DA, "vector")
        quantize_h(3 * M_TILE, half_da)
        multiply(0, 3, "scalar")
        quantize_h(half_da, DA)
        for m in range(M_TILES // 2, M_TILES):
            multiply(0, m, "scalar")
        make_do(2)
        make_do(3)
        quantize_do(2)
        quantize_do(3)
        for m in range(M_TILES):
            multiply(1, m, "scalar" if m % 2 == 1 else "vector")
